import numpy as np
import ml_dtypes


def mxq(x, axis, fmt="e4m3"):
    dtype, down = {"e4m3": (ml_dtypes.float8_e4m3fn, 7), "e5m2": (ml_dtypes.float8_e5m2, 14)}[fmt]
    v = np.moveaxis(np.asarray(x, np.float32).astype(ml_dtypes.bfloat16).astype(np.float64), axis, -1)
    blocks = v.reshape(v.shape[:-1] + (-1, 32))
    amax = np.abs(blocks).max(-1, keepdims=True)
    byte = np.maximum(np.where(amax > 0, np.frexp(amax)[1] - 1 + 127, 0) - down, 1)
    scale = np.exp2(byte - 127.0)
    codes = (blocks / scale).astype(np.float32).astype(dtype).astype(np.float64)
    return np.moveaxis((codes * scale).reshape(v.shape), -1, axis)


WIDE = False


def mx_kscale(k):
    if not WIDE:
        return np.ones(k)
    levels = np.array([10, -10, 5, -5, 0])
    a = np.random.permutation(np.resize(levels, k // 512 * 4)).reshape(k // 512, 4)
    idx = np.arange(k)
    return np.exp2(a[idx // 512, idx % 128 // 32])


BF16 = ml_dtypes.bfloat16


def bf(x):
    return np.asarray(x, np.float32).astype(BF16)


def f64(x):
    return np.asarray(x).astype(np.float64)


E2M1 = np.array([0.0, 0.5, 1.0, 1.5, 2.0, 3.0, 4.0, 6.0, -0.0, -0.5, -1.0, -1.5, -2.0, -3.0, -4.0, -6.0])


def pack_weight(w, fmt):
    k, n = w.shape
    w = f64(bf(w)).reshape(k // 32, 32, n)
    amax = np.abs(w).max(1)
    if fmt == "e4m3":
        byte = np.frexp(amax)[1] - 1 + 127 - 7
    else:
        mant, ex = np.frexp(amax / 6.0)
        byte = np.where(mant > 0.5, ex, ex - 1) + 127
    byte = np.clip(np.where(amax > 0, byte, 1), 1, 254)
    scaled = (w * np.exp2(127.0 - byte)[:, None, :]).reshape(k, n).astype(np.float32)
    by_word = np.ascontiguousarray(scaled.reshape(k // 512, 128, 4, n).transpose(0, 1, 3, 2))
    if fmt == "e4m3":
        words = by_word.astype(ml_dtypes.float8_e4m3fn).view(np.uint8)
    else:
        c = by_word.astype(ml_dtypes.float4_e2m1fn).view(np.uint8) & 0xF
        words = c[..., 0::2] | (c[..., 1::2] << 4)
    return np.ascontiguousarray(words), np.ascontiguousarray(byte.astype(np.uint8).reshape(k // 512, 16, n))


def unpack_weight(words, scales, fmt):
    g, p, n, _ = words.shape
    if fmt == "e4m3":
        vals = np.ascontiguousarray(words).view(ml_dtypes.float8_e4m3fn).astype(np.float64)
    else:
        nib = np.empty((g, p, n, 4), np.uint8)
        nib[..., 0::2] = words & 0xF
        nib[..., 1::2] = words >> 4
        vals = E2M1[nib]
    vals = vals * np.repeat(np.exp2(scales.astype(np.float64) - 127.0), 8, axis=1)[..., None]
    return vals.transpose(0, 1, 3, 2).reshape(g * 512, n)


N, C, T, V, IC = 1, 4096, 2, 128, 2048
G = (IC * T) ** 0.25


def setup_inputs():
    s = mx_kscale(C)
    u = mx_kscale(IC * T)[::T]
    x = bf(np.random.standard_normal((N, C, T, V)) * s[None, :, None, None])
    Wa = np.random.standard_normal((IC, C)) * G / np.sqrt(C) / s[None, :] * u[:, None]
    Wa_words, Wa_scales = pack_weight(Wa.T, "e4m3")
    ba = bf(np.random.standard_normal(IC) * 0.3 * G * u)
    Wb = np.random.standard_normal((IC, C)) * G / np.sqrt(C) / s[None, :] / u[:, None]
    Wb_words, Wb_scales = pack_weight(Wb.T, "e4m3")
    bb = bf(np.random.standard_normal(IC) * 0.3 * G / u)
    A = bf(np.eye(V)[None] + 0.1 * np.random.standard_normal((1, V, V)))
    alpha = bf(2.0 + 0.2 * np.random.standard_normal(1))
    return {"x": x,
            "Wa_words": Wa_words,
            "Wa_scales": Wa_scales,
            "ba": ba,
            "Wb_words": Wb_words,
            "Wb_scales": Wb_scales,
            "bb": bb,
            "A": A,
            "alpha": alpha}


def reference(x, Wa_words, Wa_scales, ba, Wb_words, Wb_scales, bb, A, alpha):
    n, c, t, v = x.shape
    wa = unpack_weight(Wa_words, Wa_scales, "e4m3").T
    wb = unpack_weight(Wb_words, Wb_scales, "e4m3").T
    ic = wa.shape[0]
    xq = mxq(f64(x), 1, "e4m3").reshape(n, c, t * v)
    qa = (wa @ xq).reshape(n, ic, t, v) + f64(ba)[None, :, None, None]
    kb = (wb @ xq).reshape(n, ic, t, v) + f64(bb)[None, :, None, None]
    Q = qa.transpose(0, 3, 1, 2).reshape(n, v, ic * t)
    K = kb.reshape(n, ic * t, v)
    Graph_B = np.tanh((mxq(Q, 2, "e4m3") @ mxq(K, 1, "e4m3")) / (ic * t))
    z = f64(A) + Graph_B * f64(alpha)
    e = np.exp(z - z.max(-1, keepdims=True))
    return e / e.sum(-1, keepdims=True)

@@ -1,0 +1,201 @@
+from contextlib import ExitStack
+
+import concourse.masks as masks
+import concourse.mybir as mybir
+
+F32 = mybir.dt.float32
+BF16 = mybir.dt.bfloat16
+I32 = mybir.dt.int32
+U8 = mybir.dt.uint8
+FP8X4 = mybir.dt.float8_e4m3fn_x4
+ACT = mybir.ActivationFunctionType
+ALU = mybir.AluOpType
+AX = mybir.AxisListType
+
+P = 128
+C = 4096
+IC = 2048
+T = 2
+V = 128
+TV = T * V
+GROUPS = C // 512
+FLOPS = 2 * 2 * IC * C * TV + 2 * V * V * IC * T
+
+
+def tile_adaptivegraphconstruction_w_kernel(
+    tc, x, Wa_words, Wa_scales, ba, Wb_words, Wb_scales, bb, A, alpha, out
+):
+    nc = tc.nc
+    words = (Wa_words, Wb_words)
+    scales = (Wa_scales, Wb_scales)
+    with ExitStack() as ctx:
+        keep = ctx.enter_context(tc.tile_pool(name="keep", bufs=1))
+        psum = ctx.enter_context(tc.psum_pool(name="psum", bufs=1))
+        ctx.enter_context(tc.manual_schedule())
+
+        stage = keep.tile([P, P], BF16, name="stage")
+        ident = keep.tile([P, P], BF16, name="ident")
+        bias = keep.tile([P, 32], F32, name="bias")
+        a_sb = keep.tile([P, V], BF16, name="a_sb")
+        alpha_bf = keep.tile([P, 1], BF16, name="alpha_bf")
+        alpha_f = keep.tile([P, 1], F32, name="alpha_f")
+        warm_in = keep.tile([P, 1], F32, name="warm_in")
+        warm_out = keep.tile([P, 1], F32, name="warm_out")
+        planes = [keep.tile([P, IC], U8, name="planes%d" % b, align_bytes=64) for b in range(4)]
+        x_raw = [keep.tile([P, 4 * TV], BF16, name="x_raw%d" % g) for g in range(GROUPS)]
+        x_grp = [keep.tile([P, 4 * TV], BF16, name="x_grp%d" % g, align_bytes=64) for g in range(GROUPS)]
+        x_codes = [keep.tile([P, TV], I32, name="x_codes%d" % g, align_bytes=64) for g in range(GROUPS)]
+        x_scales = [keep.tile([P, TV], U8, name="x_scales%d" % g, align_bytes=64) for g in range(GROUPS)]
+        w = [
+            [keep.tile([P, 1024], I32, name="w%d_%d" % (ph, g), align_bytes=64) for g in range(GROUPS)]
+            for ph in range(4)
+        ]
+        q_grp = [keep.tile([P, 2048], BF16, name="q_grp%d" % ph, align_bytes=64) for ph in range(4)]
+        q_codes = [keep.tile([P, 512], I32, name="q_codes%d" % ph, align_bytes=64) for ph in range(4)]
+        q_scales = [keep.tile([P, 512], U8, name="q_scales%d" % ph, align_bytes=64) for ph in range(4)]
+
+        nc.vector.memset(planes[0][:].bitcast(I32), 0)
+        nc.vector.memset(stage[:], 0.0)
+        nc.vector.memset(warm_in[:], 0.0)
+        for b in range(1, 4):
+            nc.vector.memset(planes[b][:].bitcast(I32), 0)
+        masks.make_identity(nc, ident[:])
+        nc.scalar.dma_start(out=stage[0:16, :], in_=ba.rearrange("(i p) -> i p", p=P))
+        nc.scalar.dma_start(out=stage[16:32, :], in_=bb.rearrange("(i p) -> i p", p=P))
+        nc.scalar.dma_start(out=a_sb[:], in_=A[0])
+        nc.scalar.dma_start(out=alpha_bf[:], in_=alpha.partition_broadcast(P))
+        nc.scalar.activation(out=warm_out[:], in_=warm_in[:], func=ACT.Tanh)
+
+        xv = x.rearrange("n (g p j) t v -> (n g) p (j t v)", p=P, j=4)
+
+        def load_x(g):
+            nc.sync.dma_start(out=x_raw[g][:], in_=xv[g])
+
+        def load_w(ph, g):
+            wsel, half = divmod(ph, 2)
+            src = words[wsel][g].rearrange("p n t -> p (n t)")[:, 4096 * half : 4096 * (half + 1)]
+            nc.sync.dma_start(out=w[ph][g][:], in_=src.bitcast(I32))
+
+        def load_scales(wsel, b):
+            for quad in (0, 2, 1, 3):
+                nc.sync.dma_start(
+                    out=planes[2 * wsel + b][32 * quad : 32 * quad + 16, :].bitcast(I32),
+                    in_=scales[wsel][4 * b : 4 * b + 4, 4 * quad : 4 * quad + 4, :].bitcast(I32),
+                )
+
+        load_x(0)
+        load_scales(0, 0)
+        for g in range(GROUPS):
+            if g > 0:
+                load_x(g)
+            if g == 4:
+                load_scales(0, 1)
+            load_w(0, g)
+        for g in range(GROUPS):
+            load_w(1, g)
+        for ph in (2, 3):
+            for g in range(GROUPS):
+                if ph == 2 and g % 4 == 0:
+                    load_scales(1, g // 4)
+                load_w(ph, g)
+
+        bt_ps = psum.tile([P, P], BF16, tag="bank7", name="bt_ps")
+        nc.tensor.transpose(bt_ps[:], stage[:], ident[:])
+
+        def quantise_x(g):
+            nc.vector.tensor_copy(
+                out=x_grp[g][:].rearrange("p (c i t) -> p c t i", i=4, t=4),
+                in_=x_raw[g][:].rearrange("p (t c i) -> p c t i", t=4, i=4),
+            )
+            nc.vector.quantize_mx(out=x_codes[g][:].bitcast(FP8X4), scales=x_scales[g][:], in_=x_grp[g][:])
+
+        def evacuate(ph, banks, j):
+            wsel, half = divmod(ph, 2)
+            grp = q_grp[ph][:].rearrange("p (j v c) -> p j v c", j=4, c=4)
+            for u in range(2):
+                i = 2 * j + u
+                src = banks[i][:].rearrange("p (t v) -> p v t", t=T)
+                dst = grp[:, j, :, 2 * u : 2 * u + 2]
+                col = 16 * wsel + 8 * half + i
+                if j % 2 == 0:
+                    nc.vector.tensor_scalar(
+                        out=dst, in0=src, scalar1=bias[:, col : col + 1], scalar2=None, op0=ALU.add
+                    )
+                else:
+                    nc.scalar.activation(
+                        out=dst, in_=src, func=ACT.Identity, bias=bias[:, col : col + 1], scale=1.0
+                    )
+
+        def quantise_q(ph, j0, j1):
+            nc.vector.quantize_mx(
+                out=q_codes[ph][:, 128 * j0 : 128 * j1].bitcast(FP8X4),
+                scales=q_scales[ph][:, 128 * j0 : 128 * j1],
+                in_=q_grp[ph][:, 512 * j0 : 512 * j1],
+            )
+
+        for ph in range(4):
+            wsel, half = divmod(ph, 2)
+            banks = [psum.tile([P, TV], F32, tag="bank%d" % i, name="acc%d_%d" % (ph, i)) for i in range(8)]
+            for g in range(GROUPS):
+                if ph == 0:
+                    quantise_x(g)
+                    if g == 0:
+                        nc.vector.tensor_copy(out=bias[:], in_=bt_ps[:, 0:32])
+                        nc.vector.tensor_copy(out=alpha_f[:], in_=alpha_bf[:])
+                blk = planes[2 * wsel + g // 4]
+                k = 4 * (g % 4)
+                for i in range(8):
+                    col = 1024 * half + 128 * i
+                    nc.tensor.matmul_mx(
+                        out=banks[i][:],
+                        lhsT=w[ph][g][:, 128 * i : 128 * (i + 1)].bitcast(FP8X4),
+                        lhsT_scale=blk[k:P, col : col + 128],
+                        rhs=x_codes[g][:].bitcast(FP8X4),
+                        rhs_scale=x_scales[g][:],
+                        start=(g == 0),
+                        stop=(g == GROUPS - 1),
+                    )
+            if ph < 3:
+                for j in range(4):
+                    evacuate(ph, banks, j)
+                quantise_q(ph, 0, 4)
+            else:
+                evacuate(ph, banks, 0)
+                evacuate(ph, banks, 1)
+                quantise_q(ph, 0, 1)
+                evacuate(ph, banks, 2)
+                evacuate(ph, banks, 3)
+                quantise_q(ph, 1, 2)
+                quantise_q(ph, 2, 3)
+                quantise_q(ph, 3, 4)
+
+        g_ps = psum.tile([P, V], F32, tag="bank0", name="g_ps")
+        for n in range(8):
+            half, j = divmod(n, 4)
+            cols = slice(128 * j, 128 * (j + 1))
+            nc.tensor.matmul_mx(
+                out=g_ps[:],
+                lhsT=q_codes[half][:, cols].bitcast(FP8X4),
+                lhsT_scale=q_scales[half][:, cols],
+                rhs=q_codes[2 + half][:, cols].bitcast(FP8X4),
+                rhs_scale=q_scales[2 + half][:, cols],
+                start=(n == 0),
+                stop=(n == 7),
+            )
+
+        th = keep.tile([P, V], F32, name="th")
+        z = keep.tile([P, V], F32, name="z")
+        e = keep.tile([P, V], F32, name="e")
+        res = keep.tile([P, V], F32, name="res")
+        negmax = keep.tile([P, 1], F32, name="negmax")
+        total = keep.tile([P, 1], F32, name="total")
+        recip = keep.tile([P, 1], F32, name="recip")
+        nc.scalar.activation(out=th[:], in_=g_ps[:], func=ACT.Tanh, scale=1.0 / (IC * T))
+        nc.vector.scalar_tensor_tensor(
+            out=z[:], in0=th[:], scalar=alpha_f[:, 0:1], in1=a_sb[:], op0=ALU.mult, op1=ALU.add
+        )
+        nc.vector.tensor_reduce(out=negmax[:], in_=z[:], axis=AX.X, op=ALU.max, negate=True)
+        nc.scalar.activation(out=e[:], in_=z[:], func=ACT.Exp, bias=negmax[:, 0:1], scale=1.0, accum_out=total[:])
+        nc.vector.reciprocal(out=recip[:], in_=total[:])
+        nc.vector.tensor_scalar(out=res[:], in0=e[:], scalar1=recip[:, 0:1], scalar2=None, op0=ALU.mult)
+        nc.sync.dma_start(out=out[0], in_=res[:])

@@ -19,7 +19,13 @@ T = 2
 V = 128
 TV = T * V
 GROUPS = C // 512
+PAIRS = IC // 256
 FLOPS = 2 * 2 * IC * C * TV + 2 * V * V * IC * T
+
+PIECES_A = [(0, 0, 4), (0, 4, 4)] + [(g, 0, PAIRS) for g in range(1, GROUPS)]
+PIECES_B = [(g, 0, PAIRS) for g in range(GROUPS - 2)] + [
+    (6, 0, 2), (7, 0, 2), (6, 2, 2), (7, 2, 2), (6, 4, 2), (7, 4, 2), (6, 6, 2), (7, 6, 1), (7, 7, 1),
+]
 
 
 def tile_adaptivegraphconstruction_w_kernel(
@@ -28,6 +34,7 @@ def tile_adaptivegraphconstruction_w_kernel(
     nc = tc.nc
     words = (Wa_words, Wb_words)
     scales = (Wa_scales, Wb_scales)
+    pieces = (PIECES_A, PIECES_B)
     with ExitStack() as ctx:
         keep = ctx.enter_context(tc.tile_pool(name="keep", bufs=1))
         psum = ctx.enter_context(tc.psum_pool(name="psum", bufs=1))
@@ -35,7 +42,7 @@ def tile_adaptivegraphconstruction_w_kernel(
 
         stage = keep.tile([P, P], BF16, name="stage")
         ident = keep.tile([P, P], BF16, name="ident")
-        bias = keep.tile([P, 32], F32, name="bias")
+        bias4 = keep.tile([P, 2 * PAIRS, 4], F32, name="bias4")
         a_sb = keep.tile([P, V], BF16, name="a_sb")
         alpha_bf = keep.tile([P, 1], BF16, name="alpha_bf")
         alpha_f = keep.tile([P, 1], F32, name="alpha_f")
@@ -47,12 +54,15 @@ def tile_adaptivegraphconstruction_w_kernel(
         x_codes = [keep.tile([P, TV], I32, name="x_codes%d" % g, align_bytes=64) for g in range(GROUPS)]
         x_scales = [keep.tile([P, TV], U8, name="x_scales%d" % g, align_bytes=64) for g in range(GROUPS)]
         w = [
-            [keep.tile([P, 1024], I32, name="w%d_%d" % (ph, g), align_bytes=64) for g in range(GROUPS)]
-            for ph in range(4)
+            [
+                keep.tile([P, 256 * n], I32, name="w%d_%d" % (wsel, i), align_bytes=64)
+                for i, (g, j0, n) in enumerate(pieces[wsel])
+            ]
+            for wsel in range(2)
         ]
-        q_grp = [keep.tile([P, 2048], BF16, name="q_grp%d" % ph, align_bytes=64) for ph in range(4)]
-        q_codes = [keep.tile([P, 512], I32, name="q_codes%d" % ph, align_bytes=64) for ph in range(4)]
-        q_scales = [keep.tile([P, 512], U8, name="q_scales%d" % ph, align_bytes=64) for ph in range(4)]
+        q_grp = [keep.tile([P, PAIRS, V, 4], BF16, name="q_grp%d" % s, align_bytes=64) for s in range(2)]
+        q_codes = [keep.tile([P, PAIRS * V], I32, name="q_codes%d" % s, align_bytes=64) for s in range(2)]
+        q_scales = [keep.tile([P, PAIRS * V], U8, name="q_scales%d" % s, align_bytes=64) for s in range(2)]
 
         nc.vector.memset(planes[0][:].bitcast(I32), 0)
         nc.vector.memset(stage[:], 0.0)
@@ -68,14 +78,6 @@ def tile_adaptivegraphconstruction_w_kernel(
 
         xv = x.rearrange("n (g p j) t v -> (n g) p (j t v)", p=P, j=4)
 
-        def load_x(g):
-            nc.sync.dma_start(out=x_raw[g][:], in_=xv[g])
-
-        def load_w(ph, g):
-            wsel, half = divmod(ph, 2)
-            src = words[wsel][g].rearrange("p n t -> p (n t)")[:, 4096 * half : 4096 * (half + 1)]
-            nc.sync.dma_start(out=w[ph][g][:], in_=src.bitcast(I32))
-
         def load_scales(wsel, b):
             for quad in (0, 2, 1, 3):
                 nc.sync.dma_start(
@@ -83,21 +85,14 @@ def tile_adaptivegraphconstruction_w_kernel(
                     in_=scales[wsel][4 * b : 4 * b + 4, 4 * quad : 4 * quad + 4, :].bitcast(I32),
                 )
 
-        load_x(0)
-        load_scales(0, 0)
-        for g in range(GROUPS):
-            if g > 0:
-                load_x(g)
-            if g == 4:
-                load_scales(0, 1)
-            load_w(0, g)
-        for g in range(GROUPS):
-            load_w(1, g)
-        for ph in (2, 3):
-            for g in range(GROUPS):
-                if ph == 2 and g % 4 == 0:
-                    load_scales(1, g // 4)
-                load_w(ph, g)
+        for wsel in range(2):
+            for i, (g, j0, n) in enumerate(pieces[wsel]):
+                if wsel == 0 and j0 == 0:
+                    nc.sync.dma_start(out=x_raw[g][:], in_=xv[g])
+                if j0 == 0 and g % 4 == 0:
+                    load_scales(wsel, g // 4)
+                src = words[wsel][g].rearrange("p n t -> p (n t)")[:, 1024 * j0 : 1024 * (j0 + n)]
+                nc.sync.dma_start(out=w[wsel][i][:], in_=src.bitcast(I32))
 
         bt_ps = psum.tile([P, P], BF16, tag="bank7", name="bt_ps")
         nc.tensor.transpose(bt_ps[:], stage[:], ident[:])
@@ -109,79 +104,113 @@ def tile_adaptivegraphconstruction_w_kernel(
             )
             nc.vector.quantize_mx(out=x_codes[g][:].bitcast(FP8X4), scales=x_scales[g][:], in_=x_grp[g][:])
 
-        def evacuate(ph, banks, j):
-            wsel, half = divmod(ph, 2)
-            grp = q_grp[ph][:].rearrange("p (j v c) -> p j v c", j=4, c=4)
-            for u in range(2):
-                i = 2 * j + u
-                src = banks[i][:].rearrange("p (t v) -> p v t", t=T)
-                dst = grp[:, j, :, 2 * u : 2 * u + 2]
-                col = 16 * wsel + 8 * half + i
-                if j % 2 == 0:
-                    nc.vector.tensor_scalar(
-                        out=dst, in0=src, scalar1=bias[:, col : col + 1], scalar2=None, op0=ALU.add
-                    )
-                else:
-                    nc.scalar.activation(
-                        out=dst, in_=src, func=ACT.Identity, bias=bias[:, col : col + 1], scale=1.0
-                    )
-
-        def quantise_q(ph, j0, j1):
-            nc.vector.quantize_mx(
-                out=q_codes[ph][:, 128 * j0 : 128 * j1].bitcast(FP8X4),
-                scales=q_scales[ph][:, 128 * j0 : 128 * j1],
-                in_=q_grp[ph][:, 512 * j0 : 512 * j1],
-            )
-
-        for ph in range(4):
-            wsel, half = divmod(ph, 2)
-            banks = [psum.tile([P, TV], F32, tag="bank%d" % i, name="acc%d_%d" % (ph, i)) for i in range(8)]
-            for g in range(GROUPS):
-                if ph == 0:
-                    quantise_x(g)
-                    if g == 0:
-                        nc.vector.tensor_copy(out=bias[:], in_=bt_ps[:, 0:32])
-                        nc.vector.tensor_copy(out=alpha_f[:], in_=alpha_bf[:])
-                blk = planes[2 * wsel + g // 4]
-                k = 4 * (g % 4)
-                for i in range(8):
-                    col = 1024 * half + 128 * i
+        def passes(wsel, i, banks):
+            g, j0, n = pieces[wsel][i]
+            blk = planes[2 * wsel + g // 4]
+            k = 4 * (g % 4)
+            for j in range(j0, j0 + n):
+                for u in range(2):
+                    local = 256 * (j - j0) + 128 * u
+                    col = 256 * j + 128 * u
                     nc.tensor.matmul_mx(
-                        out=banks[i][:],
-                        lhsT=w[ph][g][:, 128 * i : 128 * (i + 1)].bitcast(FP8X4),
+                        out=banks[j][:, TV * u : TV * (u + 1)],
+                        lhsT=w[wsel][i][:, local : local + 128].bitcast(FP8X4),
                         lhsT_scale=blk[k:P, col : col + 128],
                         rhs=x_codes[g][:].bitcast(FP8X4),
                         rhs_scale=x_scales[g][:],
-                        start=(g == 0),
-                        stop=(g == GROUPS - 1),
+                        start=(g == 0 and u == 0),
+                        stop=(g == GROUPS - 1 and u == 1),
                     )
-            if ph < 3:
-                for j in range(4):
-                    evacuate(ph, banks, j)
-                quantise_q(ph, 0, 4)
-            else:
-                evacuate(ph, banks, 0)
-                evacuate(ph, banks, 1)
-                quantise_q(ph, 0, 1)
-                evacuate(ph, banks, 2)
-                evacuate(ph, banks, 3)
-                quantise_q(ph, 1, 2)
-                quantise_q(ph, 2, 3)
-                quantise_q(ph, 3, 4)
 
-        g_ps = psum.tile([P, V], F32, tag="bank0", name="g_ps")
-        for n in range(8):
-            half, j = divmod(n, 4)
-            cols = slice(128 * j, 128 * (j + 1))
-            nc.tensor.matmul_mx(
-                out=g_ps[:],
-                lhsT=q_codes[half][:, cols].bitcast(FP8X4),
-                lhsT_scale=q_scales[half][:, cols],
-                rhs=q_codes[2 + half][:, cols].bitcast(FP8X4),
-                rhs_scale=q_scales[2 + half][:, cols],
-                start=(n == 0),
-                stop=(n == 7),
+        def evacuate(wsel, banks, j, on_vector):
+            a = PAIRS * wsel + j
+            if on_vector:
+                nc.vector.tensor_tensor(
+                    out=q_grp[wsel][:, j],
+                    in0=banks[j][:].rearrange("p (c v) -> p v c", c=4),
+                    in1=bias4[:, a : a + 1, :].to_broadcast([P, V, 4]),
+                    op=ALU.add,
+                )
+            else:
+                for u in range(2):
+                    nc.scalar.activation(
+                        out=q_grp[wsel][:, j, :, 2 * u : 2 * u + 2],
+                        in_=banks[j][:, TV * u : TV * (u + 1)].rearrange("p (t v) -> p v t", t=T),
+                        func=ACT.Identity,
+                        bias=bias4[:, a, 2 * u : 2 * u + 1],
+                        scale=1.0,
+                    )
+
+        def quantise_q(wsel, j0, j1):
+            nc.vector.quantize_mx(
+                out=q_codes[wsel][:, V * j0 : V * j1].bitcast(FP8X4),
+                scales=q_scales[wsel][:, V * j0 : V * j1],
+                in_=q_grp[wsel][:, j0:j1].rearrange("p j v c -> p (j v c)"),
             )
+
+        banks = [psum.tile([P, 2 * TV], F32, tag="bank%d" % j, name="acc0_%d" % j) for j in range(PAIRS)]
+        for i, (g, j0, n) in enumerate(PIECES_A):
+            if j0 == 0:
+                quantise_x(g)
+            if i == 0:
+                nc.vector.tensor_copy(
+                    out=bias4[:].rearrange("p a (u t) -> p (a u) t", t=2),
+                    in_=bt_ps[:, 0:32].unsqueeze(2).to_broadcast([P, 32, 2]),
+                )
+                nc.vector.tensor_copy(out=alpha_f[:], in_=alpha_bf[:])
+            passes(0, i, banks)
+        for j in range(PAIRS):
+            evacuate(0, banks, j, j not in (1, 4, 6))
+        quantise_q(0, 0, 4)
+        quantise_q(0, 4, 8)
+
+        banks = [psum.tile([P, 2 * TV], F32, tag="bank%d" % j, name="acc1_%d" % j) for j in range(PAIRS)]
+        g_box = []
+
+        def second(j):
+            if not g_box:
+                g_box.append(psum.tile([P, V], F32, tag="bank0", name="g_ps"))
+            cols = slice(V * j, V * (j + 1))
+            nc.tensor.matmul_mx(
+                out=g_box[0][:],
+                lhsT=q_codes[0][:, cols].bitcast(FP8X4),
+                lhsT_scale=q_scales[0][:, cols],
+                rhs=q_codes[1][:, cols].bitcast(FP8X4),
+                rhs_scale=q_scales[1][:, cols],
+                start=(j == 0),
+                stop=(j == PAIRS - 1),
+            )
+
+        for i in range(6):
+            passes(1, i, banks)
+        passes(1, 6, banks)
+        passes(1, 7, banks)
+        evacuate(1, banks, 0, True)
+        evacuate(1, banks, 1, False)
+        quantise_q(1, 0, 2)
+        passes(1, 8, banks)
+        passes(1, 9, banks)
+        evacuate(1, banks, 2, True)
+        evacuate(1, banks, 3, False)
+        quantise_q(1, 2, 4)
+        passes(1, 10, banks)
+        second(0)
+        second(1)
+        passes(1, 11, banks)
+        evacuate(1, banks, 4, True)
+        evacuate(1, banks, 5, False)
+        quantise_q(1, 4, 6)
+        passes(1, 12, banks)
+        second(2)
+        second(3)
+        passes(1, 13, banks)
+        evacuate(1, banks, 6, False)
+        passes(1, 14, banks)
+        evacuate(1, banks, 7, True)
+        quantise_q(1, 6, 8)
+        for j in range(4, 8):
+            second(j)
+        g_ps = g_box[0]
 
         th = keep.tile([P, V], F32, name="th")
         z = keep.tile([P, V], F32, name="z")

@@ -19,13 +19,10 @@ T = 2
 V = 128
 TV = T * V
 GROUPS = C // 512
-PAIRS = IC // 256
 FLOPS = 2 * 2 * IC * C * TV + 2 * V * V * IC * T
 
-PIECES_A = [(0, 0, 4), (0, 4, 4)] + [(g, 0, PAIRS) for g in range(1, GROUPS)]
-PIECES_B = [(g, 0, PAIRS) for g in range(GROUPS - 2)] + [
-    (6, 0, 2), (7, 0, 2), (6, 2, 2), (7, 2, 2), (6, 4, 2), (7, 4, 2), (6, 6, 2), (7, 6, 1), (7, 7, 1),
-]
+WHOLE = [(g, 0, 8) for g in range(GROUPS)]
+PIECES = [WHOLE, WHOLE, WHOLE, WHOLE[:6] + [(6, 0, 4), (7, 0, 4), (6, 4, 4), (7, 4, 2), (7, 6, 2)]]
 
 
 def tile_adaptivegraphconstruction_w_kernel(
@@ -34,7 +31,6 @@ def tile_adaptivegraphconstruction_w_kernel(
     nc = tc.nc
     words = (Wa_words, Wb_words)
     scales = (Wa_scales, Wb_scales)
-    pieces = (PIECES_A, PIECES_B)
     with ExitStack() as ctx:
         keep = ctx.enter_context(tc.tile_pool(name="keep", bufs=1))
         psum = ctx.enter_context(tc.psum_pool(name="psum", bufs=1))
@@ -42,7 +38,7 @@ def tile_adaptivegraphconstruction_w_kernel(
 
         stage = keep.tile([P, P], BF16, name="stage")
         ident = keep.tile([P, P], BF16, name="ident")
-        bias4 = keep.tile([P, 2 * PAIRS, 4], F32, name="bias4")
+        bias = keep.tile([P, 32], F32, name="bias")
         a_sb = keep.tile([P, V], BF16, name="a_sb")
         alpha_bf = keep.tile([P, 1], BF16, name="alpha_bf")
         alpha_f = keep.tile([P, 1], F32, name="alpha_f")
@@ -55,14 +51,14 @@ def tile_adaptivegraphconstruction_w_kernel(
         x_scales = [keep.tile([P, TV], U8, name="x_scales%d" % g, align_bytes=64) for g in range(GROUPS)]
         w = [
             [
-                keep.tile([P, 256 * n], I32, name="w%d_%d" % (wsel, i), align_bytes=64)
-                for i, (g, j0, n) in enumerate(pieces[wsel])
+                keep.tile([P, 128 * n], I32, name="w%d_%d" % (ph, i), align_bytes=64)
+                for i, (g, i0, n) in enumerate(PIECES[ph])
             ]
-            for wsel in range(2)
+            for ph in range(4)
         ]
-        q_grp = [keep.tile([P, PAIRS, V, 4], BF16, name="q_grp%d" % s, align_bytes=64) for s in range(2)]
-        q_codes = [keep.tile([P, PAIRS * V], I32, name="q_codes%d" % s, align_bytes=64) for s in range(2)]
-        q_scales = [keep.tile([P, PAIRS * V], U8, name="q_scales%d" % s, align_bytes=64) for s in range(2)]
+        q_grp = [keep.tile([P, 2048], BF16, name="q_grp%d" % ph, align_bytes=64) for ph in range(4)]
+        q_codes = [keep.tile([P, 512], I32, name="q_codes%d" % ph, align_bytes=64) for ph in range(4)]
+        q_scales = [keep.tile([P, 512], U8, name="q_scales%d" % ph, align_bytes=64) for ph in range(4)]
 
         nc.vector.memset(planes[0][:].bitcast(I32), 0)
         nc.vector.memset(stage[:], 0.0)
@@ -78,6 +74,16 @@ def tile_adaptivegraphconstruction_w_kernel(
 
         xv = x.rearrange("n (g p j) t v -> (n g) p (j t v)", p=P, j=4)
 
+        def load_x(g):
+            nc.sync.dma_start(out=x_raw[g][:], in_=xv[g])
+
+        def load_w(ph, i):
+            wsel, half = divmod(ph, 2)
+            g, i0, n = PIECES[ph][i]
+            first = 4096 * half + 512 * i0
+            src = words[wsel][g].rearrange("p n t -> p (n t)")[:, first : first + 512 * n]
+            nc.sync.dma_start(out=w[ph][i][:], in_=src.bitcast(I32))
+
         def load_scales(wsel, b):
             for quad in (0, 2, 1, 3):
                 nc.sync.dma_start(
@@ -85,14 +91,22 @@ def tile_adaptivegraphconstruction_w_kernel(
                     in_=scales[wsel][4 * b : 4 * b + 4, 4 * quad : 4 * quad + 4, :].bitcast(I32),
                 )
 
-        for wsel in range(2):
-            for i, (g, j0, n) in enumerate(pieces[wsel]):
-                if wsel == 0 and j0 == 0:
-                    nc.sync.dma_start(out=x_raw[g][:], in_=xv[g])
-                if j0 == 0 and g % 4 == 0:
-                    load_scales(wsel, g // 4)
-                src = words[wsel][g].rearrange("p n t -> p (n t)")[:, 1024 * j0 : 1024 * (j0 + n)]
-                nc.sync.dma_start(out=w[wsel][i][:], in_=src.bitcast(I32))
+        load_x(0)
+        load_scales(0, 0)
+        for g in range(GROUPS):
+            if g > 0:
+                load_x(g)
+            if g == 4:
+                load_scales(0, 1)
+            load_w(0, g)
+        for g in range(GROUPS):
+            load_w(1, g)
+        for g in range(GROUPS):
+            if g % 4 == 0:
+                load_scales(1, g // 4)
+            load_w(2, g)
+        for i in range(len(PIECES[3])):
+            load_w(3, i)
 
         bt_ps = psum.tile([P, P], BF16, tag="bank7", name="bt_ps")
         nc.tensor.transpose(bt_ps[:], stage[:], ident[:])
@@ -104,113 +118,90 @@ def tile_adaptivegraphconstruction_w_kernel(
             )
             nc.vector.quantize_mx(out=x_codes[g][:].bitcast(FP8X4), scales=x_scales[g][:], in_=x_grp[g][:])
 
-        def passes(wsel, i, banks):
-            g, j0, n = pieces[wsel][i]
+        def evacuate(ph, banks, j, on_vector=None):
+            wsel, half = divmod(ph, 2)
+            grp = q_grp[ph][:].rearrange("p (j v c) -> p j v c", j=4, c=4)
+            for u in range(2):
+                i = 2 * j + u
+                src = banks[i][:].rearrange("p (t v) -> p v t", t=T)
+                dst = grp[:, j, :, 2 * u : 2 * u + 2]
+                col = 16 * wsel + 8 * half + i
+                if (j % 2 == 0) if on_vector is None else on_vector:
+                    nc.vector.tensor_scalar(
+                        out=dst, in0=src, scalar1=bias[:, col : col + 1], scalar2=None, op0=ALU.add
+                    )
+                else:
+                    nc.scalar.activation(
+                        out=dst, in_=src, func=ACT.Identity, bias=bias[:, col : col + 1], scale=1.0
+                    )
+
+        def quantise_q(ph, j0, j1):
+            nc.vector.quantize_mx(
+                out=q_codes[ph][:, 128 * j0 : 128 * j1].bitcast(FP8X4),
+                scales=q_scales[ph][:, 128 * j0 : 128 * j1],
+                in_=q_grp[ph][:, 512 * j0 : 512 * j1],
+            )
+
+        def passes(ph, piece, banks):
+            wsel, half = divmod(ph, 2)
+            g, i0, n = PIECES[ph][piece]
             blk = planes[2 * wsel + g // 4]
             k = 4 * (g % 4)
-            for j in range(j0, j0 + n):
-                for u in range(2):
-                    local = 256 * (j - j0) + 128 * u
-                    col = 256 * j + 128 * u
-                    nc.tensor.matmul_mx(
-                        out=banks[j][:, TV * u : TV * (u + 1)],
-                        lhsT=w[wsel][i][:, local : local + 128].bitcast(FP8X4),
-                        lhsT_scale=blk[k:P, col : col + 128],
-                        rhs=x_codes[g][:].bitcast(FP8X4),
-                        rhs_scale=x_scales[g][:],
-                        start=(g == 0 and u == 0),
-                        stop=(g == GROUPS - 1 and u == 1),
-                    )
-
-        def evacuate(wsel, banks, j, on_vector):
-            a = PAIRS * wsel + j
-            if on_vector:
-                nc.vector.tensor_tensor(
-                    out=q_grp[wsel][:, j],
-                    in0=banks[j][:].rearrange("p (c v) -> p v c", c=4),
-                    in1=bias4[:, a : a + 1, :].to_broadcast([P, V, 4]),
-                    op=ALU.add,
+            for i in range(i0, i0 + n):
+                col = 1024 * half + 128 * i
+                nc.tensor.matmul_mx(
+                    out=banks[i][:],
+                    lhsT=w[ph][piece][:, 128 * (i - i0) : 128 * (i - i0 + 1)].bitcast(FP8X4),
+                    lhsT_scale=blk[k:P, col : col + 128],
+                    rhs=x_codes[g][:].bitcast(FP8X4),
+                    rhs_scale=x_scales[g][:],
+                    start=(g == 0),
+                    stop=(g == GROUPS - 1),
                 )
-            else:
-                for u in range(2):
-                    nc.scalar.activation(
-                        out=q_grp[wsel][:, j, :, 2 * u : 2 * u + 2],
-                        in_=banks[j][:, TV * u : TV * (u + 1)].rearrange("p (t v) -> p v t", t=T),
-                        func=ACT.Identity,
-                        bias=bias4[:, a, 2 * u : 2 * u + 1],
-                        scale=1.0,
-                    )
 
-        def quantise_q(wsel, j0, j1):
-            nc.vector.quantize_mx(
-                out=q_codes[wsel][:, V * j0 : V * j1].bitcast(FP8X4),
-                scales=q_scales[wsel][:, V * j0 : V * j1],
-                in_=q_grp[wsel][:, j0:j1].rearrange("p j v c -> p (j v c)"),
-            )
-
-        banks = [psum.tile([P, 2 * TV], F32, tag="bank%d" % j, name="acc0_%d" % j) for j in range(PAIRS)]
-        for i, (g, j0, n) in enumerate(PIECES_A):
-            if j0 == 0:
-                quantise_x(g)
-            if i == 0:
-                nc.vector.tensor_copy(
-                    out=bias4[:].rearrange("p a (u t) -> p (a u) t", t=2),
-                    in_=bt_ps[:, 0:32].unsqueeze(2).to_broadcast([P, 32, 2]),
-                )
-                nc.vector.tensor_copy(out=alpha_f[:], in_=alpha_bf[:])
-            passes(0, i, banks)
-        for j in range(PAIRS):
-            evacuate(0, banks, j, j not in (1, 4, 6))
-        quantise_q(0, 0, 4)
-        quantise_q(0, 4, 8)
-
-        banks = [psum.tile([P, 2 * TV], F32, tag="bank%d" % j, name="acc1_%d" % j) for j in range(PAIRS)]
-        g_box = []
-
-        def second(j):
-            if not g_box:
-                g_box.append(psum.tile([P, V], F32, tag="bank0", name="g_ps"))
-            cols = slice(V * j, V * (j + 1))
+        def second(g_ps, n):
+            half, j = divmod(n, 4)
+            cols = slice(128 * j, 128 * (j + 1))
             nc.tensor.matmul_mx(
-                out=g_box[0][:],
-                lhsT=q_codes[0][:, cols].bitcast(FP8X4),
-                lhsT_scale=q_scales[0][:, cols],
-                rhs=q_codes[1][:, cols].bitcast(FP8X4),
-                rhs_scale=q_scales[1][:, cols],
-                start=(j == 0),
-                stop=(j == PAIRS - 1),
+                out=g_ps[:],
+                lhsT=q_codes[half][:, cols].bitcast(FP8X4),
+                lhsT_scale=q_scales[half][:, cols],
+                rhs=q_codes[2 + half][:, cols].bitcast(FP8X4),
+                rhs_scale=q_scales[2 + half][:, cols],
+                start=(n == 0),
+                stop=(n == 7),
             )
 
-        for i in range(6):
-            passes(1, i, banks)
-        passes(1, 6, banks)
-        passes(1, 7, banks)
-        evacuate(1, banks, 0, True)
-        evacuate(1, banks, 1, False)
-        quantise_q(1, 0, 2)
-        passes(1, 8, banks)
-        passes(1, 9, banks)
-        evacuate(1, banks, 2, True)
-        evacuate(1, banks, 3, False)
-        quantise_q(1, 2, 4)
-        passes(1, 10, banks)
-        second(0)
-        second(1)
-        passes(1, 11, banks)
-        evacuate(1, banks, 4, True)
-        evacuate(1, banks, 5, False)
-        quantise_q(1, 4, 6)
-        passes(1, 12, banks)
-        second(2)
-        second(3)
-        passes(1, 13, banks)
-        evacuate(1, banks, 6, False)
-        passes(1, 14, banks)
-        evacuate(1, banks, 7, True)
-        quantise_q(1, 6, 8)
-        for j in range(4, 8):
-            second(j)
-        g_ps = g_box[0]
+        for ph in range(3):
+            banks = [psum.tile([P, TV], F32, tag="bank%d" % i, name="acc%d_%d" % (ph, i)) for i in range(8)]
+            for g in range(GROUPS):
+                if ph == 0:
+                    quantise_x(g)
+                    if g == 0:
+                        nc.vector.tensor_copy(out=bias[:], in_=bt_ps[:, 0:32])
+                        nc.vector.tensor_copy(out=alpha_f[:], in_=alpha_bf[:])
+                passes(ph, g, banks)
+            for j in range(4):
+                evacuate(ph, banks, j)
+            quantise_q(ph, 0, 4)
+
+        banks = [psum.tile([P, TV], F32, tag="bank%d" % i, name="acc3_%d" % i) for i in range(8)]
+        for piece in range(8):
+            passes(3, piece, banks)
+        evacuate(3, banks, 0)
+        evacuate(3, banks, 1)
+        quantise_q(3, 0, 2)
+        passes(3, 8, banks)
+        g_ps = psum.tile([P, V], F32, tag="bank0", name="g_ps")
+        for n in range(4):
+            second(g_ps, n)
+        passes(3, 9, banks)
+        evacuate(3, banks, 2, False)
+        passes(3, 10, banks)
+        evacuate(3, banks, 3, True)
+        quantise_q(3, 2, 4)
+        for n in range(4, 8):
+            second(g_ps, n)
 
         th = keep.tile([P, V], F32, name="th")
         z = keep.tile([P, V], F32, name="z")

@@ -19,10 +19,13 @@ T = 2
 V = 128
 TV = T * V
 GROUPS = C // 512
+PAIRS = IC // 256
 FLOPS = 2 * 2 * IC * C * TV + 2 * V * V * IC * T
 
-WHOLE = [(g, 0, 8) for g in range(GROUPS)]
-PIECES = [WHOLE, WHOLE, WHOLE, WHOLE[:6] + [(6, 0, 4), (7, 0, 4), (6, 4, 4), (7, 4, 2), (7, 6, 2)]]
+PIECES_A = [(0, 0, 4), (0, 4, 4)] + [(g, 0, PAIRS) for g in range(1, GROUPS)]
+PIECES_B = [(g, 0, PAIRS) for g in range(GROUPS - 2)] + [
+    (6, 0, 2), (7, 0, 2), (6, 2, 2), (7, 2, 2), (6, 4, 2), (7, 4, 2), (6, 6, 2), (7, 6, 1), (7, 7, 1),
+]
 
 
 def tile_adaptivegraphconstruction_w_kernel(
@@ -31,6 +34,7 @@ def tile_adaptivegraphconstruction_w_kernel(
     nc = tc.nc
     words = (Wa_words, Wb_words)
     scales = (Wa_scales, Wb_scales)
+    pieces = (PIECES_A, PIECES_B)
     with ExitStack() as ctx:
         keep = ctx.enter_context(tc.tile_pool(name="keep", bufs=1))
         psum = ctx.enter_context(tc.psum_pool(name="psum", bufs=1))
@@ -38,7 +42,7 @@ def tile_adaptivegraphconstruction_w_kernel(
 
         stage = keep.tile([P, P], BF16, name="stage")
         ident = keep.tile([P, P], BF16, name="ident")
-        bias = keep.tile([P, 32], F32, name="bias")
+        bias4 = keep.tile([P, 2 * PAIRS, 4], F32, name="bias4")
         a_sb = keep.tile([P, V], BF16, name="a_sb")
         alpha_bf = keep.tile([P, 1], BF16, name="alpha_bf")
         alpha_f = keep.tile([P, 1], F32, name="alpha_f")
@@ -51,14 +55,14 @@ def tile_adaptivegraphconstruction_w_kernel(
         x_scales = [keep.tile([P, TV], U8, name="x_scales%d" % g, align_bytes=64) for g in range(GROUPS)]
         w = [
             [
-                keep.tile([P, 128 * n], I32, name="w%d_%d" % (ph, i), align_bytes=64)
-                for i, (g, i0, n) in enumerate(PIECES[ph])
+                keep.tile([P, 256 * n], I32, name="w%d_%d" % (wsel, i), align_bytes=64)
+                for i, (g, j0, n) in enumerate(pieces[wsel])
             ]
-            for ph in range(4)
+            for wsel in range(2)
         ]
-        q_grp = [keep.tile([P, 2048], BF16, name="q_grp%d" % ph, align_bytes=64) for ph in range(4)]
-        q_codes = [keep.tile([P, 512], I32, name="q_codes%d" % ph, align_bytes=64) for ph in range(4)]
-        q_scales = [keep.tile([P, 512], U8, name="q_scales%d" % ph, align_bytes=64) for ph in range(4)]
+        q_grp = [keep.tile([P, PAIRS, V, 4], BF16, name="q_grp%d" % s, align_bytes=64) for s in range(2)]
+        q_codes = [keep.tile([P, PAIRS * V], I32, name="q_codes%d" % s, align_bytes=64) for s in range(2)]
+        q_scales = [keep.tile([P, PAIRS * V], U8, name="q_scales%d" % s, align_bytes=64) for s in range(2)]
 
         nc.vector.memset(planes[0][:].bitcast(I32), 0)
         nc.vector.memset(stage[:], 0.0)
@@ -74,16 +78,6 @@ def tile_adaptivegraphconstruction_w_kernel(
 
         xv = x.rearrange("n (g p j) t v -> (n g) p (j t v)", p=P, j=4)
 
-        def load_x(g):
-            nc.sync.dma_start(out=x_raw[g][:], in_=xv[g])
-
-        def load_w(ph, i):
-            wsel, half = divmod(ph, 2)
-            g, i0, n = PIECES[ph][i]
-            first = 4096 * half + 512 * i0
-            src = words[wsel][g].rearrange("p n t -> p (n t)")[:, first : first + 512 * n]
-            nc.sync.dma_start(out=w[ph][i][:], in_=src.bitcast(I32))
-
         def load_scales(wsel, b):
             for quad in (0, 2, 1, 3):
                 nc.sync.dma_start(
@@ -91,22 +85,16 @@ def tile_adaptivegraphconstruction_w_kernel(
                     in_=scales[wsel][4 * b : 4 * b + 4, 4 * quad : 4 * quad + 4, :].bitcast(I32),
                 )
 
-        load_x(0)
+        scales_after = {(0, 1): (0, 1), (0, 5): (1, 0), (1, 0): (1, 1)}
         load_scales(0, 0)
-        for g in range(GROUPS):
-            if g > 0:
-                load_x(g)
-            if g == 4:
-                load_scales(0, 1)
-            load_w(0, g)
-        for g in range(GROUPS):
-            load_w(1, g)
-        for g in range(GROUPS):
-            if g % 4 == 0:
-                load_scales(1, g // 4)
-            load_w(2, g)
-        for i in range(len(PIECES[3])):
-            load_w(3, i)
+        for wsel in range(2):
+            for i, (g, j0, n) in enumerate(pieces[wsel]):
+                if wsel == 0 and j0 == 0:
+                    nc.sync.dma_start(out=x_raw[g][:], in_=xv[g])
+                src = words[wsel][g].rearrange("p n t -> p (n t)")[:, 1024 * j0 : 1024 * (j0 + n)]
+                nc.sync.dma_start(out=w[wsel][i][:], in_=src.bitcast(I32))
+                if (wsel, i) in scales_after:
+                    load_scales(*scales_after[(wsel, i)])
 
         bt_ps = psum.tile([P, P], BF16, tag="bank7", name="bt_ps")
         nc.tensor.transpose(bt_ps[:], stage[:], ident[:])
@@ -118,90 +106,113 @@ def tile_adaptivegraphconstruction_w_kernel(
             )
             nc.vector.quantize_mx(out=x_codes[g][:].bitcast(FP8X4), scales=x_scales[g][:], in_=x_grp[g][:])
 
-        def evacuate(ph, banks, j, on_vector=None):
-            wsel, half = divmod(ph, 2)
-            grp = q_grp[ph][:].rearrange("p (j v c) -> p j v c", j=4, c=4)
-            for u in range(2):
-                i = 2 * j + u
-                src = banks[i][:].rearrange("p (t v) -> p v t", t=T)
-                dst = grp[:, j, :, 2 * u : 2 * u + 2]
-                col = 16 * wsel + 8 * half + i
-                if (j % 2 == 0) if on_vector is None else on_vector:
-                    nc.vector.tensor_scalar(
-                        out=dst, in0=src, scalar1=bias[:, col : col + 1], scalar2=None, op0=ALU.add
-                    )
-                else:
-                    nc.scalar.activation(
-                        out=dst, in_=src, func=ACT.Identity, bias=bias[:, col : col + 1], scale=1.0
-                    )
-
-        def quantise_q(ph, j0, j1):
-            nc.vector.quantize_mx(
-                out=q_codes[ph][:, 128 * j0 : 128 * j1].bitcast(FP8X4),
-                scales=q_scales[ph][:, 128 * j0 : 128 * j1],
-                in_=q_grp[ph][:, 512 * j0 : 512 * j1],
-            )
-
-        def passes(ph, piece, banks):
-            wsel, half = divmod(ph, 2)
-            g, i0, n = PIECES[ph][piece]
+        def passes(wsel, i, banks):
+            g, j0, n = pieces[wsel][i]
             blk = planes[2 * wsel + g // 4]
             k = 4 * (g % 4)
-            for i in range(i0, i0 + n):
-                col = 1024 * half + 128 * i
-                nc.tensor.matmul_mx(
-                    out=banks[i][:],
-                    lhsT=w[ph][piece][:, 128 * (i - i0) : 128 * (i - i0 + 1)].bitcast(FP8X4),
-                    lhsT_scale=blk[k:P, col : col + 128],
-                    rhs=x_codes[g][:].bitcast(FP8X4),
-                    rhs_scale=x_scales[g][:],
-                    start=(g == 0),
-                    stop=(g == GROUPS - 1),
-                )
+            for j in range(j0, j0 + n):
+                for u in range(2):
+                    local = 256 * (j - j0) + 128 * u
+                    col = 256 * j + 128 * u
+                    nc.tensor.matmul_mx(
+                        out=banks[j][:, TV * u : TV * (u + 1)],
+                        lhsT=w[wsel][i][:, local : local + 128].bitcast(FP8X4),
+                        lhsT_scale=blk[k:P, col : col + 128],
+                        rhs=x_codes[g][:].bitcast(FP8X4),
+                        rhs_scale=x_scales[g][:],
+                        start=(g == 0 and u == 0),
+                        stop=(g == GROUPS - 1 and u == 1),
+                    )
 
-        def second(g_ps, n):
-            half, j = divmod(n, 4)
-            cols = slice(128 * j, 128 * (j + 1))
-            nc.tensor.matmul_mx(
-                out=g_ps[:],
-                lhsT=q_codes[half][:, cols].bitcast(FP8X4),
-                lhsT_scale=q_scales[half][:, cols],
-                rhs=q_codes[2 + half][:, cols].bitcast(FP8X4),
-                rhs_scale=q_scales[2 + half][:, cols],
-                start=(n == 0),
-                stop=(n == 7),
+        def evacuate(wsel, banks, j, on_vector):
+            a = PAIRS * wsel + j
+            if on_vector:
+                nc.vector.tensor_tensor(
+                    out=q_grp[wsel][:, j],
+                    in0=banks[j][:].rearrange("p (c v) -> p v c", c=4),
+                    in1=bias4[:, a : a + 1, :].to_broadcast([P, V, 4]),
+                    op=ALU.add,
+                )
+            else:
+                for u in range(2):
+                    nc.scalar.activation(
+                        out=q_grp[wsel][:, j, :, 2 * u : 2 * u + 2],
+                        in_=banks[j][:, TV * u : TV * (u + 1)].rearrange("p (t v) -> p v t", t=T),
+                        func=ACT.Identity,
+                        bias=bias4[:, a, 2 * u : 2 * u + 1],
+                        scale=1.0,
+                    )
+
+        def quantise_q(wsel, j0, j1):
+            nc.vector.quantize_mx(
+                out=q_codes[wsel][:, V * j0 : V * j1].bitcast(FP8X4),
+                scales=q_scales[wsel][:, V * j0 : V * j1],
+                in_=q_grp[wsel][:, j0:j1].rearrange("p j v c -> p (j v c)"),
             )
 
-        for ph in range(3):
-            banks = [psum.tile([P, TV], F32, tag="bank%d" % i, name="acc%d_%d" % (ph, i)) for i in range(8)]
-            for g in range(GROUPS):
-                if ph == 0:
-                    quantise_x(g)
-                    if g == 0:
-                        nc.vector.tensor_copy(out=bias[:], in_=bt_ps[:, 0:32])
-                        nc.vector.tensor_copy(out=alpha_f[:], in_=alpha_bf[:])
-                passes(ph, g, banks)
-            for j in range(4):
-                evacuate(ph, banks, j)
-            quantise_q(ph, 0, 4)
+        banks = [psum.tile([P, 2 * TV], F32, tag="bank%d" % j, name="acc0_%d" % j) for j in range(PAIRS)]
+        for i, (g, j0, n) in enumerate(PIECES_A):
+            if j0 == 0:
+                quantise_x(g)
+            if i == 0:
+                nc.vector.tensor_copy(
+                    out=bias4[:].rearrange("p a (u t) -> p (a u) t", t=2),
+                    in_=bt_ps[:, 0:32].unsqueeze(2).to_broadcast([P, 32, 2]),
+                )
+                nc.vector.tensor_copy(out=alpha_f[:], in_=alpha_bf[:])
+            passes(0, i, banks)
+        for j in range(PAIRS):
+            evacuate(0, banks, j, j not in (1, 4, 6))
+        quantise_q(0, 0, 4)
+        quantise_q(0, 4, 8)
 
-        banks = [psum.tile([P, TV], F32, tag="bank%d" % i, name="acc3_%d" % i) for i in range(8)]
-        for piece in range(8):
-            passes(3, piece, banks)
-        evacuate(3, banks, 0)
-        evacuate(3, banks, 1)
-        quantise_q(3, 0, 2)
-        passes(3, 8, banks)
-        g_ps = psum.tile([P, V], F32, tag="bank0", name="g_ps")
-        for n in range(4):
-            second(g_ps, n)
-        passes(3, 9, banks)
-        evacuate(3, banks, 2, False)
-        passes(3, 10, banks)
-        evacuate(3, banks, 3, True)
-        quantise_q(3, 2, 4)
-        for n in range(4, 8):
-            second(g_ps, n)
+        banks = [psum.tile([P, 2 * TV], F32, tag="bank%d" % j, name="acc1_%d" % j) for j in range(PAIRS)]
+        g_box = []
+
+        def second(j):
+            if not g_box:
+                g_box.append(psum.tile([P, V], F32, tag="bank0", name="g_ps"))
+            cols = slice(V * j, V * (j + 1))
+            nc.tensor.matmul_mx(
+                out=g_box[0][:],
+                lhsT=q_codes[0][:, cols].bitcast(FP8X4),
+                lhsT_scale=q_scales[0][:, cols],
+                rhs=q_codes[1][:, cols].bitcast(FP8X4),
+                rhs_scale=q_scales[1][:, cols],
+                start=(j == 0),
+                stop=(j == PAIRS - 1),
+            )
+
+        for i in range(6):
+            passes(1, i, banks)
+        passes(1, 6, banks)
+        passes(1, 7, banks)
+        evacuate(1, banks, 0, True)
+        evacuate(1, banks, 1, False)
+        quantise_q(1, 0, 2)
+        passes(1, 8, banks)
+        passes(1, 9, banks)
+        evacuate(1, banks, 2, True)
+        evacuate(1, banks, 3, False)
+        quantise_q(1, 2, 4)
+        passes(1, 10, banks)
+        second(0)
+        second(1)
+        passes(1, 11, banks)
+        evacuate(1, banks, 4, True)
+        evacuate(1, banks, 5, False)
+        quantise_q(1, 4, 6)
+        passes(1, 12, banks)
+        second(2)
+        second(3)
+        passes(1, 13, banks)
+        evacuate(1, banks, 6, False)
+        passes(1, 14, banks)
+        evacuate(1, banks, 7, True)
+        quantise_q(1, 6, 8)
+        for j in range(4, 8):
+            second(j)
+        g_ps = g_box[0]
 
         th = keep.tile([P, V], F32, name="th")
         z = keep.tile([P, V], F32, name="z")

@@ -19,13 +19,10 @@ T = 2
 V = 128
 TV = T * V
 GROUPS = C // 512
-PAIRS = IC // 256
 FLOPS = 2 * 2 * IC * C * TV + 2 * V * V * IC * T
 
-PIECES_A = [(0, 0, 4), (0, 4, 4)] + [(g, 0, PAIRS) for g in range(1, GROUPS)]
-PIECES_B = [(g, 0, PAIRS) for g in range(GROUPS - 2)] + [
-    (6, 0, 2), (7, 0, 2), (6, 2, 2), (7, 2, 2), (6, 4, 2), (7, 4, 2), (6, 6, 2), (7, 6, 1), (7, 7, 1),
-]
+WHOLE = [(g, 0, 8) for g in range(GROUPS)]
+PIECES = [WHOLE, WHOLE, WHOLE, WHOLE[:6] + [(6, 0, 4), (7, 0, 4), (6, 4, 4), (7, 4, 2), (7, 6, 2)]]
 
 
 def tile_adaptivegraphconstruction_w_kernel(
@@ -34,7 +31,6 @@ def tile_adaptivegraphconstruction_w_kernel(
     nc = tc.nc
     words = (Wa_words, Wb_words)
     scales = (Wa_scales, Wb_scales)
-    pieces = (PIECES_A, PIECES_B)
     with ExitStack() as ctx:
         keep = ctx.enter_context(tc.tile_pool(name="keep", bufs=1))
         psum = ctx.enter_context(tc.psum_pool(name="psum", bufs=1))
@@ -42,7 +38,7 @@ def tile_adaptivegraphconstruction_w_kernel(
 
         stage = keep.tile([P, P], BF16, name="stage")
         ident = keep.tile([P, P], BF16, name="ident")
-        bias4 = keep.tile([P, 2 * PAIRS, 4], F32, name="bias4")
+        bias = keep.tile([P, 32], F32, name="bias")
         a_sb = keep.tile([P, V], BF16, name="a_sb")
         alpha_bf = keep.tile([P, 1], BF16, name="alpha_bf")
         alpha_f = keep.tile([P, 1], F32, name="alpha_f")
@@ -55,14 +51,14 @@ def tile_adaptivegraphconstruction_w_kernel(
         x_scales = [keep.tile([P, TV], U8, name="x_scales%d" % g, align_bytes=64) for g in range(GROUPS)]
         w = [
             [
-                keep.tile([P, 256 * n], I32, name="w%d_%d" % (wsel, i), align_bytes=64)
-                for i, (g, j0, n) in enumerate(pieces[wsel])
+                keep.tile([P, 128 * n], I32, name="w%d_%d" % (ph, i), align_bytes=64)
+                for i, (g, i0, n) in enumerate(PIECES[ph])
             ]
-            for wsel in range(2)
+            for ph in range(4)
         ]
-        q_grp = [keep.tile([P, PAIRS, V, 4], BF16, name="q_grp%d" % s, align_bytes=64) for s in range(2)]
-        q_codes = [keep.tile([P, PAIRS * V], I32, name="q_codes%d" % s, align_bytes=64) for s in range(2)]
-        q_scales = [keep.tile([P, PAIRS * V], U8, name="q_scales%d" % s, align_bytes=64) for s in range(2)]
+        q_grp = [keep.tile([P, 2048], BF16, name="q_grp%d" % ph, align_bytes=64) for ph in range(4)]
+        q_codes = [keep.tile([P, 512], I32, name="q_codes%d" % ph, align_bytes=64) for ph in range(4)]
+        q_scales = [keep.tile([P, 512], U8, name="q_scales%d" % ph, align_bytes=64) for ph in range(4)]
 
         nc.vector.memset(planes[0][:].bitcast(I32), 0)
         nc.vector.memset(stage[:], 0.0)
@@ -78,6 +74,16 @@ def tile_adaptivegraphconstruction_w_kernel(
 
         xv = x.rearrange("n (g p j) t v -> (n g) p (j t v)", p=P, j=4)
 
+        def load_x(g):
+            nc.sync.dma_start(out=x_raw[g][:], in_=xv[g])
+
+        def load_w(ph, i):
+            wsel, half = divmod(ph, 2)
+            g, i0, n = PIECES[ph][i]
+            first = 4096 * half + 512 * i0
+            src = words[wsel][g].rearrange("p n t -> p (n t)")[:, first : first + 512 * n]
+            nc.sync.dma_start(out=w[ph][i][:], in_=src.bitcast(I32))
+
         def load_scales(wsel, b):
             for quad in (0, 2, 1, 3):
                 nc.sync.dma_start(
@@ -85,134 +91,122 @@ def tile_adaptivegraphconstruction_w_kernel(
                     in_=scales[wsel][4 * b : 4 * b + 4, 4 * quad : 4 * quad + 4, :].bitcast(I32),
                 )
 
-        scales_after = {(0, 1): (0, 1), (0, 5): (1, 0), (1, 0): (1, 1)}
+        load_x(0)
         load_scales(0, 0)
-        for wsel in range(2):
-            for i, (g, j0, n) in enumerate(pieces[wsel]):
-                if wsel == 0 and j0 == 0:
-                    nc.sync.dma_start(out=x_raw[g][:], in_=xv[g])
-                src = words[wsel][g].rearrange("p n t -> p (n t)")[:, 1024 * j0 : 1024 * (j0 + n)]
-                nc.sync.dma_start(out=w[wsel][i][:], in_=src.bitcast(I32))
-                if (wsel, i) in scales_after:
-                    load_scales(*scales_after[(wsel, i)])
+        for g in range(1, GROUPS):
+            load_x(g)
+        for g in range(GROUPS):
+            if g == 4:
+                load_scales(0, 1)
+            load_w(0, g)
+        for g in range(GROUPS):
+            load_w(1, g)
+        for g in range(GROUPS):
+            if g % 4 == 0:
+                load_scales(1, g // 4)
+            load_w(2, g)
+        for i in range(len(PIECES[3])):
+            load_w(3, i)
 
         bt_ps = psum.tile([P, P], BF16, tag="bank7", name="bt_ps")
         nc.tensor.transpose(bt_ps[:], stage[:], ident[:])
 
-        def quantise_x(g):
+        def regroup_x(g):
             nc.vector.tensor_copy(
                 out=x_grp[g][:].rearrange("p (c i t) -> p c t i", i=4, t=4),
                 in_=x_raw[g][:].rearrange("p (t c i) -> p c t i", t=4, i=4),
             )
+
+        def quantise_x(g):
             nc.vector.quantize_mx(out=x_codes[g][:].bitcast(FP8X4), scales=x_scales[g][:], in_=x_grp[g][:])
 
-        def passes(wsel, i, banks):
-            g, j0, n = pieces[wsel][i]
+        regroup_x(0)
+        for g in range(1, GROUPS):
+            regroup_x(g)
+            quantise_x(g - 1)
+        quantise_x(GROUPS - 1)
+        nc.vector.tensor_copy(out=bias[:], in_=bt_ps[:, 0:32])
+        nc.vector.tensor_copy(out=alpha_f[:], in_=alpha_bf[:])
+
+        def evacuate(ph, banks, j, on_vector=None):
+            wsel, half = divmod(ph, 2)
+            grp = q_grp[ph][:].rearrange("p (j v c) -> p j v c", j=4, c=4)
+            for u in range(2):
+                i = 2 * j + u
+                src = banks[i][:].rearrange("p (t v) -> p v t", t=T)
+                dst = grp[:, j, :, 2 * u : 2 * u + 2]
+                col = 16 * wsel + 8 * half + i
+                if (j % 2 == 0) if on_vector is None else on_vector:
+                    nc.vector.tensor_scalar(
+                        out=dst, in0=src, scalar1=bias[:, col : col + 1], scalar2=None, op0=ALU.add
+                    )
+                else:
+                    nc.scalar.activation(
+                        out=dst, in_=src, func=ACT.Identity, bias=bias[:, col : col + 1], scale=1.0
+                    )
+
+        def quantise_q(ph, j0, j1):
+            nc.vector.quantize_mx(
+                out=q_codes[ph][:, 128 * j0 : 128 * j1].bitcast(FP8X4),
+                scales=q_scales[ph][:, 128 * j0 : 128 * j1],
+                in_=q_grp[ph][:, 512 * j0 : 512 * j1],
+            )
+
+        def passes(ph, piece, banks):
+            wsel, half = divmod(ph, 2)
+            g, i0, n = PIECES[ph][piece]
             blk = planes[2 * wsel + g // 4]
             k = 4 * (g % 4)
-            for j in range(j0, j0 + n):
-                for u in range(2):
-                    local = 256 * (j - j0) + 128 * u
-                    col = 256 * j + 128 * u
-                    nc.tensor.matmul_mx(
-                        out=banks[j][:, TV * u : TV * (u + 1)],
-                        lhsT=w[wsel][i][:, local : local + 128].bitcast(FP8X4),
-                        lhsT_scale=blk[k:P, col : col + 128],
-                        rhs=x_codes[g][:].bitcast(FP8X4),
-                        rhs_scale=x_scales[g][:],
-                        start=(g == 0 and u == 0),
-                        stop=(g == GROUPS - 1 and u == 1),
-                    )
-
-        def evacuate(wsel, banks, j, on_vector):
-            a = PAIRS * wsel + j
-            if on_vector:
-                nc.vector.tensor_tensor(
-                    out=q_grp[wsel][:, j],
-                    in0=banks[j][:].rearrange("p (c v) -> p v c", c=4),
-                    in1=bias4[:, a : a + 1, :].to_broadcast([P, V, 4]),
-                    op=ALU.add,
+            for i in range(i0, i0 + n):
+                col = 1024 * half + 128 * i
+                nc.tensor.matmul_mx(
+                    out=banks[i][:],
+                    lhsT=w[ph][piece][:, 128 * (i - i0) : 128 * (i - i0 + 1)].bitcast(FP8X4),
+                    lhsT_scale=blk[k:P, col : col + 128],
+                    rhs=x_codes[g][:].bitcast(FP8X4),
+                    rhs_scale=x_scales[g][:],
+                    start=(g == 0),
+                    stop=(g == GROUPS - 1),
                 )
-            else:
-                for u in range(2):
-                    nc.scalar.activation(
-                        out=q_grp[wsel][:, j, :, 2 * u : 2 * u + 2],
-                        in_=banks[j][:, TV * u : TV * (u + 1)].rearrange("p (t v) -> p v t", t=T),
-                        func=ACT.Identity,
-                        bias=bias4[:, a, 2 * u : 2 * u + 1],
-                        scale=1.0,
-                    )
 
-        def quantise_q(wsel, j0, j1):
-            nc.vector.quantize_mx(
-                out=q_codes[wsel][:, V * j0 : V * j1].bitcast(FP8X4),
-                scales=q_scales[wsel][:, V * j0 : V * j1],
-                in_=q_grp[wsel][:, j0:j1].rearrange("p j v c -> p (j v c)"),
-            )
-
-        banks = [psum.tile([P, 2 * TV], F32, tag="bank%d" % j, name="acc0_%d" % j) for j in range(PAIRS)]
-        for i, (g, j0, n) in enumerate(PIECES_A):
-            if j0 == 0:
-                quantise_x(g)
-            if i == 0:
-                nc.vector.tensor_copy(
-                    out=bias4[:].rearrange("p a (u t) -> p (a u) t", t=2),
-                    in_=bt_ps[:, 0:32].unsqueeze(2).to_broadcast([P, 32, 2]),
-                )
-                nc.vector.tensor_copy(out=alpha_f[:], in_=alpha_bf[:])
-            passes(0, i, banks)
-        for j in range(PAIRS):
-            evacuate(0, banks, j, j not in (1, 4, 6))
-        quantise_q(0, 0, 4)
-        quantise_q(0, 4, 8)
-
-        banks = [psum.tile([P, 2 * TV], F32, tag="bank%d" % j, name="acc1_%d" % j) for j in range(PAIRS)]
-        g_box = []
-
-        def second(j):
-            if not g_box:
-                g_box.append(psum.tile([P, V], F32, tag="bank0", name="g_ps"))
-            cols = slice(V * j, V * (j + 1))
+        def second(g_ps, n):
+            half, j = divmod(n, 4)
+            cols = slice(128 * j, 128 * (j + 1))
             nc.tensor.matmul_mx(
-                out=g_box[0][:],
-                lhsT=q_codes[0][:, cols].bitcast(FP8X4),
-                lhsT_scale=q_scales[0][:, cols],
-                rhs=q_codes[1][:, cols].bitcast(FP8X4),
-                rhs_scale=q_scales[1][:, cols],
-                start=(j == 0),
-                stop=(j == PAIRS - 1),
+                out=g_ps[:],
+                lhsT=q_codes[half][:, cols].bitcast(FP8X4),
+                lhsT_scale=q_scales[half][:, cols],
+                rhs=q_codes[2 + half][:, cols].bitcast(FP8X4),
+                rhs_scale=q_scales[2 + half][:, cols],
+                start=(n == 0),
+                stop=(n == 7),
             )
 
-        for i in range(6):
-            passes(1, i, banks)
-        passes(1, 6, banks)
-        passes(1, 7, banks)
-        evacuate(1, banks, 0, True)
-        evacuate(1, banks, 1, False)
-        quantise_q(1, 0, 2)
-        passes(1, 8, banks)
-        passes(1, 9, banks)
-        evacuate(1, banks, 2, True)
-        evacuate(1, banks, 3, False)
-        quantise_q(1, 2, 4)
-        passes(1, 10, banks)
-        second(0)
-        second(1)
-        passes(1, 11, banks)
-        evacuate(1, banks, 4, True)
-        evacuate(1, banks, 5, False)
-        quantise_q(1, 4, 6)
-        passes(1, 12, banks)
-        second(2)
-        second(3)
-        passes(1, 13, banks)
-        evacuate(1, banks, 6, False)
-        passes(1, 14, banks)
-        evacuate(1, banks, 7, True)
-        quantise_q(1, 6, 8)
-        for j in range(4, 8):
-            second(j)
-        g_ps = g_box[0]
+        for ph in range(3):
+            banks = [psum.tile([P, TV], F32, tag="bank%d" % i, name="acc%d_%d" % (ph, i)) for i in range(8)]
+            for g in range(GROUPS):
+                passes(ph, g, banks)
+            for j in range(4):
+                evacuate(ph, banks, j)
+            quantise_q(ph, 0, 4)
+
+        banks = [psum.tile([P, TV], F32, tag="bank%d" % i, name="acc3_%d" % i) for i in range(8)]
+        for piece in range(8):
+            passes(3, piece, banks)
+        evacuate(3, banks, 0)
+        evacuate(3, banks, 1)
+        quantise_q(3, 0, 2)
+        passes(3, 8, banks)
+        g_ps = psum.tile([P, V], F32, tag="bank0", name="g_ps")
+        for n in range(4):
+            second(g_ps, n)
+        passes(3, 9, banks)
+        evacuate(3, banks, 2, False)
+        passes(3, 10, banks)
+        evacuate(3, banks, 3, True)
+        quantise_q(3, 2, 4)
+        for n in range(4, 8):
+            second(g_ps, n)
 
         th = keep.tile([P, V], F32, name="th")
         z = keep.tile([P, V], F32, name="z")

from contextlib import ExitStack

import concourse.masks as masks
import concourse.mybir as mybir

F32 = mybir.dt.float32
BF16 = mybir.dt.bfloat16
I32 = mybir.dt.int32
U8 = mybir.dt.uint8
FP8X4 = mybir.dt.float8_e4m3fn_x4
ACT = mybir.ActivationFunctionType
ALU = mybir.AluOpType
AX = mybir.AxisListType

P = 128
C = 4096
IC = 2048
T = 2
V = 128
TV = T * V
GROUPS = C // 512
FLOPS = 2 * 2 * IC * C * TV + 2 * V * V * IC * T

WHOLE = [(g, 0, 8) for g in range(GROUPS)]
PIECES = [WHOLE, WHOLE, WHOLE, WHOLE[:6] + [(6, 0, 4), (7, 0, 4), (6, 4, 4), (7, 4, 2), (7, 6, 2)]]


def tile_adaptivegraphconstruction_w_kernel(
    tc, x, Wa_words, Wa_scales, ba, Wb_words, Wb_scales, bb, A, alpha, out
):
    nc = tc.nc
    words = (Wa_words, Wb_words)
    scales = (Wa_scales, Wb_scales)
    with ExitStack() as ctx:
        keep = ctx.enter_context(tc.tile_pool(name="keep", bufs=1))
        psum = ctx.enter_context(tc.psum_pool(name="psum", bufs=1))
        ctx.enter_context(tc.manual_schedule())

        stage = keep.tile([P, P], BF16, name="stage")
        ident = keep.tile([P, P], BF16, name="ident")
        bias = keep.tile([P, 32], F32, name="bias")
        a_sb = keep.tile([P, V], BF16, name="a_sb")
        alpha_bf = keep.tile([P, 1], BF16, name="alpha_bf")
        alpha_f = keep.tile([P, 1], F32, name="alpha_f")
        warm_in = keep.tile([P, 1], F32, name="warm_in")
        warm_out = keep.tile([P, 1], F32, name="warm_out")
        planes = [keep.tile([P, IC], U8, name="planes%d" % b, align_bytes=64) for b in range(4)]
        x_raw = [keep.tile([P, 4 * TV], BF16, name="x_raw%d" % g) for g in range(GROUPS)]
        x_grp = [keep.tile([P, 4 * TV], BF16, name="x_grp%d" % g, align_bytes=64) for g in range(GROUPS)]
        x_codes = [keep.tile([P, TV], I32, name="x_codes%d" % g, align_bytes=64) for g in range(GROUPS)]
        x_scales = [keep.tile([P, TV], U8, name="x_scales%d" % g, align_bytes=64) for g in range(GROUPS)]
        w = [
            [
                keep.tile([P, 128 * n], I32, name="w%d_%d" % (ph, i), align_bytes=64)
                for i, (g, i0, n) in enumerate(PIECES[ph])
            ]
            for ph in range(4)
        ]
        q_grp = [keep.tile([P, 2048], BF16, name="q_grp%d" % ph, align_bytes=64) for ph in range(4)]
        q_codes = [keep.tile([P, 512], I32, name="q_codes%d" % ph, align_bytes=64) for ph in range(4)]
        q_scales = [keep.tile([P, 512], U8, name="q_scales%d" % ph, align_bytes=64) for ph in range(4)]

        nc.vector.memset(planes[0][:].bitcast(I32), 0)
        nc.vector.memset(stage[:], 0.0)
        nc.vector.memset(warm_in[:], 0.0)
        for b in range(1, 4):
            nc.vector.memset(planes[b][:].bitcast(I32), 0)
        masks.make_identity(nc, ident[:])
        nc.scalar.dma_start(out=stage[0:16, :], in_=ba.rearrange("(i p) -> i p", p=P))
        nc.scalar.dma_start(out=stage[16:32, :], in_=bb.rearrange("(i p) -> i p", p=P))
        nc.scalar.dma_start(out=a_sb[:], in_=A[0])
        nc.scalar.dma_start(out=alpha_bf[:], in_=alpha.partition_broadcast(P))
        nc.scalar.activation(out=warm_out[:], in_=warm_in[:], func=ACT.Tanh)

        xv = x.rearrange("n (g p j) t v -> (n g) p (j t v)", p=P, j=4)

        def load_x(g):
            nc.sync.dma_start(out=x_raw[g][:], in_=xv[g])

        def load_w(ph, i):
            wsel, half = divmod(ph, 2)
            g, i0, n = PIECES[ph][i]
            first = 4096 * half + 512 * i0
            src = words[wsel][g].rearrange("p n t -> p (n t)")[:, first : first + 512 * n]
            nc.sync.dma_start(out=w[ph][i][:], in_=src.bitcast(I32))

        def load_scales(wsel, b):
            for quad in (0, 2, 1, 3):
                nc.sync.dma_start(
                    out=planes[2 * wsel + b][32 * quad : 32 * quad + 16, :].bitcast(I32),
                    in_=scales[wsel][4 * b : 4 * b + 4, 4 * quad : 4 * quad + 4, :].bitcast(I32),
                )

        load_x(0)
        load_scales(0, 0)
        for g in range(1, GROUPS):
            load_x(g)
        for g in range(GROUPS):
            if g == 4:
                load_scales(0, 1)
            load_w(0, g)
        for g in range(GROUPS):
            load_w(1, g)
        for g in range(GROUPS):
            if g % 4 == 0:
                load_scales(1, g // 4)
            load_w(2, g)
        for i in range(len(PIECES[3])):
            load_w(3, i)

        bt_ps = psum.tile([P, P], BF16, tag="bank7", name="bt_ps")
        nc.tensor.transpose(bt_ps[:], stage[:], ident[:])

        def regroup_x(g):
            nc.vector.tensor_copy(
                out=x_grp[g][:].rearrange("p (c i t) -> p c t i", i=4, t=4),
                in_=x_raw[g][:].rearrange("p (t c i) -> p c t i", t=4, i=4),
            )

        def quantise_x(g):
            nc.vector.quantize_mx(out=x_codes[g][:].bitcast(FP8X4), scales=x_scales[g][:], in_=x_grp[g][:])

        regroup_x(0)
        for g in range(1, GROUPS):
            regroup_x(g)
            quantise_x(g - 1)
        quantise_x(GROUPS - 1)
        nc.vector.tensor_copy(out=bias[:], in_=bt_ps[:, 0:32])
        nc.vector.tensor_copy(out=alpha_f[:], in_=alpha_bf[:])

        def evacuate(ph, banks, j, on_vector=None):
            wsel, half = divmod(ph, 2)
            grp = q_grp[ph][:].rearrange("p (j v c) -> p j v c", j=4, c=4)
            for u in range(2):
                i = 2 * j + u
                src = banks[i][:].rearrange("p (t v) -> p v t", t=T)
                dst = grp[:, j, :, 2 * u : 2 * u + 2]
                col = 16 * wsel + 8 * half + i
                if (j % 2 == 0) if on_vector is None else on_vector:
                    nc.vector.tensor_scalar(
                        out=dst, in0=src, scalar1=bias[:, col : col + 1], scalar2=None, op0=ALU.add
                    )
                else:
                    nc.scalar.activation(
                        out=dst, in_=src, func=ACT.Identity, bias=bias[:, col : col + 1], scale=1.0
                    )

        def quantise_q(ph, j0, j1):
            nc.vector.quantize_mx(
                out=q_codes[ph][:, 128 * j0 : 128 * j1].bitcast(FP8X4),
                scales=q_scales[ph][:, 128 * j0 : 128 * j1],
                in_=q_grp[ph][:, 512 * j0 : 512 * j1],
            )

        def passes(ph, piece, banks):
            wsel, half = divmod(ph, 2)
            g, i0, n = PIECES[ph][piece]
            blk = planes[2 * wsel + g // 4]
            k = 4 * (g % 4)
            for i in range(i0, i0 + n):
                col = 1024 * half + 128 * i
                nc.tensor.matmul_mx(
                    out=banks[i][:],
                    lhsT=w[ph][piece][:, 128 * (i - i0) : 128 * (i - i0 + 1)].bitcast(FP8X4),
                    lhsT_scale=blk[k:P, col : col + 128],
                    rhs=x_codes[g][:].bitcast(FP8X4),
                    rhs_scale=x_scales[g][:],
                    start=(g == 0),
                    stop=(g == GROUPS - 1),
                )

        def second(g_ps, n):
            half, j = divmod(n, 4)
            cols = slice(128 * j, 128 * (j + 1))
            nc.tensor.matmul_mx(
                out=g_ps[:],
                lhsT=q_codes[half][:, cols].bitcast(FP8X4),
                lhsT_scale=q_scales[half][:, cols],
                rhs=q_codes[2 + half][:, cols].bitcast(FP8X4),
                rhs_scale=q_scales[2 + half][:, cols],
                start=(n == 0),
                stop=(n == 7),
            )

        for ph in range(3):
            banks = [psum.tile([P, TV], F32, tag="bank%d" % i, name="acc%d_%d" % (ph, i)) for i in range(8)]
            for g in range(GROUPS):
                passes(ph, g, banks)
            for j in range(4):
                evacuate(ph, banks, j)
            quantise_q(ph, 0, 4)

        banks = [psum.tile([P, TV], F32, tag="bank%d" % i, name="acc3_%d" % i) for i in range(8)]
        for piece in range(8):
            passes(3, piece, banks)
        evacuate(3, banks, 0)
        evacuate(3, banks, 1)
        quantise_q(3, 0, 2)
        passes(3, 8, banks)
        g_ps = psum.tile([P, V], F32, tag="bank0", name="g_ps")
        for n in range(4):
            second(g_ps, n)
        passes(3, 9, banks)
        evacuate(3, banks, 2, False)
        passes(3, 10, banks)
        evacuate(3, banks, 3, True)
        quantise_q(3, 2, 4)
        for n in range(4, 8):
            second(g_ps, n)

        th = keep.tile([P, V], F32, name="th")
        z = keep.tile([P, V], F32, name="z")
        e = keep.tile([P, V], F32, name="e")
        res = keep.tile([P, V], F32, name="res")
        negmax = keep.tile([P, 1], F32, name="negmax")
        total = keep.tile([P, 1], F32, name="total")
        recip = keep.tile([P, 1], F32, name="recip")
        nc.scalar.activation(out=th[:], in_=g_ps[:], func=ACT.Tanh, scale=1.0 / (IC * T))
        nc.vector.scalar_tensor_tensor(
            out=z[:], in0=th[:], scalar=alpha_f[:, 0:1], in1=a_sb[:], op0=ALU.mult, op1=ALU.add
        )
        nc.vector.tensor_reduce(out=negmax[:], in_=z[:], axis=AX.X, op=ALU.max, negate=True)
        nc.scalar.activation(out=e[:], in_=z[:], func=ACT.Exp, bias=negmax[:, 0:1], scale=1.0, accum_out=total[:])
        nc.vector.reciprocal(out=recip[:], in_=total[:])
        nc.vector.tensor_scalar(out=res[:], in0=e[:], scalar1=recip[:, 0:1], scalar2=None, op0=ALU.mult)
        nc.sync.dma_start(out=out[0], in_=res[:])
